import numpy as np
import ml_dtypes


def mxq(x, axis, fmt="e4m3"):
    dtype, down = {"e4m3": (ml_dtypes.float8_e4m3fn, 7), "e5m2": (ml_dtypes.float8_e5m2, 14)}[fmt]
    v = np.moveaxis(np.asarray(x, np.float32).astype(ml_dtypes.bfloat16).astype(np.float64), axis, -1)
    blocks = v.reshape(v.shape[:-1] + (-1, 32))
    amax = np.abs(blocks).max(-1, keepdims=True)
    byte = np.maximum(np.where(amax > 0, np.frexp(amax)[1] - 1 + 127, 0) - down, 1)
    scale = np.exp2(byte - 127.0)
    codes = (blocks / scale).astype(np.float32).astype(dtype).astype(np.float64)
    return np.moveaxis((codes * scale).reshape(v.shape), -1, axis)


WIDE = False


def mx_kscale(k):
    if not WIDE:
        return np.ones(k)
    levels = np.array([30, -30])
    if k % 512:
        return np.exp2(np.random.permutation(np.resize(levels, k // 32))).repeat(32)
    a = np.empty((k // 512, 16))
    for p in range(k // 512):
        a[p, :8] = np.random.permutation(np.resize(levels, 8))
        for g in range(8):
            far = levels[np.abs(levels - a[p, g]) >= 10]
            a[p, g + 8] = far[np.random.randint(len(far))]
    return np.exp2(a.ravel()).repeat(32)


BF16 = ml_dtypes.bfloat16


def bf(x):
    return np.asarray(x, np.float32).astype(BF16)


def f64(x):
    return np.asarray(x).astype(np.float64)


B, S, D, E = 4, 512, 1024, 1024
THETA = 10000.0


def rope_tables():
    inv = 1.0 / THETA ** (np.arange(0, E, 2).astype(np.float64) / E)
    ang = np.outer(np.arange(S).astype(np.float64), inv)
    return np.cos(ang), np.sin(ang)


def rotate(u, cos, sin):
    ur, ui = u[..., 0::2], u[..., 1::2]
    return np.stack([ur * cos - ui * sin, ur * sin + ui * cos], axis=-1).reshape(B, S, E)


def setup_inputs():
    s = mx_kscale(D)
    return {"x": bf(np.random.standard_normal((B, S, D)) * s),
            "wq": bf(np.random.standard_normal((E, D)) / np.sqrt(D) / s),
            "wk": bf(np.random.standard_normal((E, D)) / np.sqrt(D) / s)}


def reference(x, wq, wk):
    xm = mxq(f64(x), 2, "e5m2")
    xq = xm @ mxq(f64(wq), 1, "e5m2").T
    xk = xm @ mxq(f64(wk), 1, "e5m2").T
    cos, sin = rope_tables()
    return rotate(xq, cos, sin), rotate(xk, cos, sin)

@@ -1,0 +1,192 @@
+import math
+from contextlib import ExitStack
+
+import concourse.mybir as mybir
+from concourse.masks import make_identity
+
+B, S, D, E = 4, 512, 1024, 1024
+THETA = 10000.0
+FLOPS = 2 * (B * S) * D * (2 * E)
+
+F32 = mybir.dt.float32
+BF16 = mybir.dt.bfloat16
+I32 = mybir.dt.int32
+U32 = mybir.dt.uint32
+U8 = mybir.dt.uint8
+FP8X4 = mybir.dt.float8_e5m2_x4
+ALU = mybir.AluOpType
+ACT = mybir.ActivationFunctionType
+
+P = 128
+PASSES = D // 512
+PAIRS = E // 2
+TT = S // P
+NTILES = B * TT
+
+
+def tile_attention_pa_kernel(tc, x, wq, wk, out_0, out_1):
+    nc = tc.nc
+    ws_dram = (wq, wk)
+    outs = (out_0, out_1)
+
+    with ExitStack() as ctx:
+        const = ctx.enter_context(tc.tile_pool(name="const", bufs=1))
+        raw = ctx.enter_context(tc.tile_pool(name="raw", bufs=1))
+        keep = ctx.enter_context(tc.tile_pool(name="keep", bufs=1))
+        stage = ctx.enter_context(tc.tile_pool(name="stage", bufs=2))
+        work = ctx.enter_context(tc.tile_pool(name="work", bufs=3))
+        tpp = ctx.enter_context(tc.psum_pool(name="tpp", bufs=2))
+        accp = ctx.enter_context(tc.psum_pool(name="accp", bufs=6))
+
+        theta = const.tile([P, PAIRS], F32, name="theta")
+        nc.vector.memset(theta[:, 0:1], 1.0)
+        scratch = const.tile([P, 1], F32, name="scratch")
+        nc.scalar.activation(out=scratch[:], in_=theta[:, 0:1], func=ACT.Sin)
+        ident = const.tile([P, P], F32, name="ident")
+        make_identity(nc, ident[:])
+        t_int = const.tile([P, TT], I32, name="t_int")
+        nc.gpsimd.iota(t_int[:], pattern=[[P, TT]], base=0, channel_multiplier=1)
+
+        order = [(jt, b) for jt in range(TT) for b in range(B)]
+        x_raw = []
+        for n in range(NTILES):
+            x_raw.append(raw.tile([P, D], BF16, name="xr%d" % n))
+        w_raw = {}
+        for w in range(2):
+            for j in range(2):
+                for m in range(4):
+                    w_raw[(w, j, m)] = raw.tile([P, D], BF16, name="wr%d_%d_%d" % (w, j, m))
+
+        def load_x(n):
+            jt, b = order[n]
+            nc.sync.dma_start(out=x_raw[n][:], in_=x[b, jt * P : (jt + 1) * P, :])
+
+        def load_w(w, j):
+            view = ws_dram[w].rearrange("(m q j) k -> j m q k", q=P, j=2)
+            for m in range(4):
+                nc.sync.dma_start(out=w_raw[(w, j, m)][:], in_=view[j, m])
+
+        load_x(0)
+        load_w(0, 0)
+        load_w(0, 1)
+        load_x(1)
+        load_w(1, 0)
+        load_w(1, 1)
+        for n in range(2, NTILES):
+            load_x(n)
+
+        n = 1
+        while n < PAIRS:
+            nc.vector.tensor_scalar(
+                out=theta[:, n : 2 * n], in0=theta[:, 0:n],
+                scalar1=THETA ** (-n / PAIRS), scalar2=None, op0=ALU.mult,
+            )
+            n *= 2
+        halfpi = const.tile([P, 1], F32, name="halfpi")
+        nc.vector.tensor_scalar(out=halfpi[:], in0=theta[:, 0:1], scalar1=math.pi / 2, scalar2=None, op0=ALU.mult)
+        t_turns = const.tile([P, TT], F32, name="t_turns")
+        nc.vector.tensor_scalar(out=t_turns[:], in0=t_int[:], scalar1=1.0 / (2 * math.pi), scalar2=None, op0=ALU.mult)
+
+        table = const.tile([P, TT, 3, PAIRS], F32, name="table")
+
+        def make_table(jt):
+            turns = stage.tile([P, PAIRS], F32, name="turns")
+            nc.vector.tensor_scalar(out=turns[:], in0=theta[:], scalar1=t_turns[:, jt : jt + 1], scalar2=None, op0=ALU.mult)
+            whole = stage.tile([P, PAIRS], I32, name="whole")
+            nc.vector.tensor_copy(out=whole[:], in_=turns[:])
+            frac = stage.tile([P, PAIRS], F32, name="frac")
+            nc.vector.tensor_tensor(out=frac[:], in0=turns[:], in1=whole[:], op=ALU.subtract)
+            nc.scalar.activation(out=table[:, jt, 2, :], in_=frac[:], func=ACT.Sin, scale=2 * math.pi)
+            nc.scalar.activation(out=table[:, jt, 0, :], in_=frac[:], func=ACT.Sin, scale=-2 * math.pi)
+            absf = stage.tile([P, PAIRS], F32, name="absf")
+            nc.scalar.activation(out=absf[:], in_=frac[:], func=ACT.Abs)
+            nc.scalar.activation(out=table[:, jt, 1, :], in_=absf[:], func=ACT.Sin, scale=-2 * math.pi, bias=halfpi[:])
+
+        def turn(src, dst_words):
+            words = src[:].bitcast(F32)
+            tp = tpp.tile([P, PASSES, 2, P], F32, name="tp")
+            for g in range(PASSES):
+                for u in range(2):
+                    nc.tensor.transpose(tp[:, g, u, :], words[:, 256 * g + u : 256 * (g + 1) : 2], ident[:])
+            nc.scalar.copy(out=dst_words, in_=tp[:].rearrange("p g u c -> p g c u"))
+
+        x_codes = []
+        x_scales = []
+        for n in range(NTILES):
+            x_codes.append(keep.tile([P, PASSES * P], U32, name="xc%d" % n, align_bytes=64))
+            x_scales.append(keep.tile([P, PASSES * P], U8, name="xs%d" % n, align_bytes=64))
+        w_codes = {}
+        w_scales = {}
+        for w in range(2):
+            for j in range(2):
+                w_codes[(w, j)] = keep.tile([P, PASSES, PAIRS], U32, name="wc%d_%d" % (w, j), align_bytes=64)
+                w_scales[(w, j)] = keep.tile([P, PASSES, PAIRS], U8, name="ws%d_%d" % (w, j), align_bytes=64)
+
+        def prep_x(n):
+            gx = stage.tile([P, PASSES, P, 4], BF16, name="gx", align_bytes=64)
+            turn(x_raw[n], gx[:].bitcast(F32))
+            nc.vector.quantize_mx(
+                out=x_codes[n][:].bitcast(FP8X4), scales=x_scales[n][:],
+                in_=gx[:].rearrange("p g c t -> p (g c t)"),
+            )
+
+        def prep_w(w, j):
+            gw = stage.tile([P, PASSES, PAIRS, 4], BF16, name="gw", align_bytes=64)
+            for m in range(4):
+                turn(w_raw[(w, j, m)], gw[:].bitcast(F32)[:, :, m * P : (m + 1) * P, :])
+            for g in range(PASSES):
+                nc.vector.quantize_mx(
+                    out=w_codes[(w, j)][:, g, :].bitcast(FP8X4), scales=w_scales[(w, j)][:, g, :],
+                    in_=gw[:, g].rearrange("p c t -> p (c t)"),
+                )
+
+        def project(n, w, j):
+            acc = accp.tile([P, PAIRS], F32, name="acc")
+            for g in range(PASSES):
+                cols = slice(g * P, (g + 1) * P)
+                nc.tensor.matmul_mx(
+                    out=acc[:],
+                    lhsT=x_codes[n][:, cols].bitcast(FP8X4), lhsT_scale=x_scales[n][:, cols],
+                    rhs=w_codes[(w, j)][:, g, :].bitcast(FP8X4), rhs_scale=w_scales[(w, j)][:, g, :],
+                    start=(g == 0), stop=(g == PASSES - 1),
+                )
+            return acc
+
+        def unit(n, w):
+            jt, b = order[n]
+            real = project(n, w, 0)
+            pa = work.tile([P, 2, PAIRS], F32, name="pa")
+            nc.vector.tensor_tensor(
+                out=pa[:], in0=real[:].unsqueeze(1).to_broadcast([P, 2, PAIRS]), in1=table[:, jt, 1:3, :], op=ALU.mult,
+            )
+            imag = project(n, w, 1)
+            pb = work.tile([P, 2, PAIRS], F32, name="pb")
+            nc.vector.tensor_tensor(
+                out=pb[:], in0=imag[:].unsqueeze(1).to_broadcast([P, 2, PAIRS]), in1=table[:, jt, 0:2, :], op=ALU.mult,
+            )
+            rot = work.tile([P, PAIRS, 2], F32, name="rot")
+            nc.gpsimd.tensor_tensor(
+                out=rot[:], in0=pa[:].rearrange("p j i -> p i j"), in1=pb[:].rearrange("p j i -> p i j"), op=ALU.add,
+            )
+            nc.sync.dma_start(out=outs[w][b, jt * P : (jt + 1) * P, :], in_=rot[:].rearrange("p i j -> p (i j)"))
+
+        make_table(0)
+        prep_x(0)
+        prep_w(0, 0)
+        prep_w(0, 1)
+        prep_x(1)
+        unit(0, 0)
+        prep_w(1, 0)
+        unit(1, 0)
+        prep_w(1, 1)
+        prep_x(2)
+        unit(0, 1)
+        prep_x(3)
+        unit(1, 1)
+        for n in range(2, NTILES):
+            if n + 2 < NTILES:
+                prep_x(n + 2)
+            if n % B == 2 and n // B + 1 < TT:
+                make_table(n // B + 1)
+            unit(n, 0)
+            unit(n, 1)

@@ -20,6 +20,8 @@ ACT = mybir.ActivationFunctionType
 P = 128
 PASSES = D // 512
 PAIRS = E // 2
+BANK = 512
+HALF = BANK // 2
 TT = S // P
 NTILES = B * TT
 
@@ -53,18 +55,18 @@ def tile_attention_pa_kernel(tc, x, wq, wk, out_0, out_1):
             x_raw.append(raw.tile([P, D], BF16, name="xr%d" % n))
         w_raw = {}
         for w in range(2):
-            for j in range(2):
+            for k in range(2):
                 for m in range(4):
-                    w_raw[(w, j, m)] = raw.tile([P, D], BF16, name="wr%d_%d_%d" % (w, j, m))
+                    w_raw[(w, k, m)] = raw.tile([P, D], BF16, name="wr%d_%d_%d" % (w, k, m))
 
         def load_x(n):
             jt, b = order[n]
             nc.sync.dma_start(out=x_raw[n][:], in_=x[b, jt * P : (jt + 1) * P, :])
 
-        def load_w(w, j):
-            view = ws_dram[w].rearrange("(m q j) k -> j m q k", q=P, j=2)
+        def load_w(w, k):
+            view = ws_dram[w].rearrange("(k mm q j) d -> k mm j q d", k=2, mm=2, q=P, j=2)
             for m in range(4):
-                nc.sync.dma_start(out=w_raw[(w, j, m)][:], in_=view[j, m])
+                nc.sync.dma_start(out=w_raw[(w, k, m)][:], in_=view[k, m % 2, 1 - m // 2])
 
         load_x(0)
         load_w(0, 0)
@@ -87,20 +89,23 @@ def tile_attention_pa_kernel(tc, x, wq, wk, out_0, out_1):
         t_turns = const.tile([P, TT], F32, name="t_turns")
         nc.vector.tensor_scalar(out=t_turns[:], in0=t_int[:], scalar1=1.0 / (2 * math.pi), scalar2=None, op0=ALU.mult)
 
-        table = const.tile([P, TT, 3, PAIRS], F32, name="table")
+        table = const.tile([P, TT, 2, PAIRS, 2], F32, name="table")
 
-        def make_table(jt):
+        def make_table(jt, copier):
             turns = stage.tile([P, PAIRS], F32, name="turns")
             nc.vector.tensor_scalar(out=turns[:], in0=theta[:], scalar1=t_turns[:, jt : jt + 1], scalar2=None, op0=ALU.mult)
             whole = stage.tile([P, PAIRS], I32, name="whole")
             nc.vector.tensor_copy(out=whole[:], in_=turns[:])
             frac = stage.tile([P, PAIRS], F32, name="frac")
             nc.vector.tensor_tensor(out=frac[:], in0=turns[:], in1=whole[:], op=ALU.subtract)
-            nc.scalar.activation(out=table[:, jt, 2, :], in_=frac[:], func=ACT.Sin, scale=2 * math.pi)
-            nc.scalar.activation(out=table[:, jt, 0, :], in_=frac[:], func=ACT.Sin, scale=-2 * math.pi)
+            trig = stage.tile([P, 3, PAIRS], F32, name="trig")
             absf = stage.tile([P, PAIRS], F32, name="absf")
             nc.scalar.activation(out=absf[:], in_=frac[:], func=ACT.Abs)
-            nc.scalar.activation(out=table[:, jt, 1, :], in_=absf[:], func=ACT.Sin, scale=-2 * math.pi, bias=halfpi[:])
+            nc.scalar.activation(out=trig[:, 1, :], in_=absf[:], func=ACT.Sin, scale=-2 * math.pi, bias=halfpi[:])
+            nc.scalar.activation(out=trig[:, 0, :], in_=frac[:], func=ACT.Sin, scale=-2 * math.pi)
+            nc.scalar.activation(out=trig[:, 2, :], in_=frac[:], func=ACT.Sin, scale=2 * math.pi)
+            for h in range(2):
+                copier(out=table[:, jt, h], in_=trig[:, h : h + 2, :].rearrange("p r i -> p i r"))
 
         def turn(src, dst_words):
             words = src[:].bitcast(F32)
@@ -118,9 +123,9 @@ def tile_attention_pa_kernel(tc, x, wq, wk, out_0, out_1):
         w_codes = {}
         w_scales = {}
         for w in range(2):
-            for j in range(2):
-                w_codes[(w, j)] = keep.tile([P, PASSES, PAIRS], U32, name="wc%d_%d" % (w, j), align_bytes=64)
-                w_scales[(w, j)] = keep.tile([P, PASSES, PAIRS], U8, name="ws%d_%d" % (w, j), align_bytes=64)
+            for k in range(2):
+                w_codes[(w, k)] = keep.tile([P, PASSES, BANK], U32, name="wc%d_%d" % (w, k), align_bytes=64)
+                w_scales[(w, k)] = keep.tile([P, PASSES, BANK], U8, name="ws%d_%d" % (w, k), align_bytes=64)
 
         def prep_x(n):
             gx = stage.tile([P, PASSES, P, 4], BF16, name="gx", align_bytes=64)
@@ -131,7 +136,7 @@ def tile_attention_pa_kernel(tc, x, wq, wk, out_0, out_1):
             )
 
         def prep_w(w, j):
-            gw = stage.tile([P, PASSES, PAIRS, 4], BF16, name="gw", align_bytes=64)
+            gw = stage.tile([P, PASSES, BANK, 4], BF16, name="gw", align_bytes=64)
             for m in range(4):
                 turn(w_raw[(w, j, m)], gw[:].bitcast(F32)[:, :, m * P : (m + 1) * P, :])
             for g in range(PASSES):
@@ -141,7 +146,7 @@ def tile_attention_pa_kernel(tc, x, wq, wk, out_0, out_1):
                 )
 
         def project(n, w, j):
-            acc = accp.tile([P, PAIRS], F32, name="acc")
+            acc = accp.tile([P, BANK], F32, name="acc")
             for g in range(PASSES):
                 cols = slice(g * P, (g + 1) * P)
                 nc.tensor.matmul_mx(
@@ -154,23 +159,21 @@ def tile_attention_pa_kernel(tc, x, wq, wk, out_0, out_1):
 
         def unit(n, w):
             jt, b = order[n]
-            real = project(n, w, 0)
-            pa = work.tile([P, 2, PAIRS], F32, name="pa")
-            nc.vector.tensor_tensor(
-                out=pa[:], in0=real[:].unsqueeze(1).to_broadcast([P, 2, PAIRS]), in1=table[:, jt, 1:3, :], op=ALU.mult,
-            )
-            imag = project(n, w, 1)
-            pb = work.tile([P, 2, PAIRS], F32, name="pb")
-            nc.vector.tensor_tensor(
-                out=pb[:], in0=imag[:].unsqueeze(1).to_broadcast([P, 2, PAIRS]), in1=table[:, jt, 0:2, :], op=ALU.mult,
-            )
-            rot = work.tile([P, PAIRS, 2], F32, name="rot")
-            nc.gpsimd.tensor_tensor(
-                out=rot[:], in0=pa[:].rearrange("p j i -> p i j"), in1=pb[:].rearrange("p j i -> p i j"), op=ALU.add,
-            )
-            nc.sync.dma_start(out=outs[w][b, jt * P : (jt + 1) * P, :], in_=rot[:].rearrange("p i j -> p (i j)"))
+            prod = work.tile([P, 2, 2, HALF, 2], F32, name="prod")
+            for k in range(2):
+                acc = project(n, w, k)
+                nc.vector.tensor_tensor(
+                    out=prod[:, k],
+                    in0=acc[:].rearrange("p (h i) -> p h i", h=2).unsqueeze(3).to_broadcast([P, 2, HALF, 2]),
+                    in1=table[:, jt, :, k * HALF : (k + 1) * HALF, :],
+                    op=ALU.mult,
+                )
+            rot = work.tile([P, 2, BANK], F32, name="rot")
+            halves = prod[:].rearrange("p k h i r -> p k h (i r)")
+            nc.gpsimd.tensor_tensor(out=rot[:], in0=halves[:, :, 0, :], in1=halves[:, :, 1, :], op=ALU.add)
+            nc.sync.dma_start(out=outs[w][b, jt * P : (jt + 1) * P, :], in_=rot[:].rearrange("p k e -> p (k e)"))
 
-        make_table(0)
+        make_table(0, nc.vector.tensor_copy)
         prep_x(0)
         prep_w(0, 0)
         prep_w(0, 1)
@@ -187,6 +190,6 @@ def tile_attention_pa_kernel(tc, x, wq, wk, out_0, out_1):
             if n + 2 < NTILES:
                 prep_x(n + 2)
             if n % B == 2 and n // B + 1 < TT:
-                make_table(n // B + 1)
+                make_table(n // B + 1, nc.scalar.copy)
             unit(n, 0)
             unit(n, 1)

@@ -24,57 +24,61 @@ BANK = 512
 HALF = BANK // 2
 TT = S // P
 NTILES = B * TT
+RAW = 8
+FIRST = 8
+VECTOR_COPIES = 3
+TURNS_A_UNIT = 3
 
 
 def tile_attention_pa_kernel(tc, x, wq, wk, out_0, out_1):
     nc = tc.nc
-    ws_dram = (wq, wk)
+    weights = (wq, wk)
     outs = (out_0, out_1)
 
     with ExitStack() as ctx:
         const = ctx.enter_context(tc.tile_pool(name="const", bufs=1))
-        raw = ctx.enter_context(tc.tile_pool(name="raw", bufs=1))
+        raw = ctx.enter_context(tc.tile_pool(name="raw", bufs=RAW))
         keep = ctx.enter_context(tc.tile_pool(name="keep", bufs=1))
         stage = ctx.enter_context(tc.tile_pool(name="stage", bufs=2))
+        once = ctx.enter_context(tc.tile_pool(name="once", bufs=1))
         work = ctx.enter_context(tc.tile_pool(name="work", bufs=3))
-        tpp = ctx.enter_context(tc.psum_pool(name="tpp", bufs=2))
-        accp = ctx.enter_context(tc.psum_pool(name="accp", bufs=6))
+        tpp = ctx.enter_context(tc.psum_pool(name="tpp", bufs=4))
+        accp = ctx.enter_context(tc.psum_pool(name="accp", bufs=4))
+        ctx.enter_context(tc.manual_schedule())
+
+        vcopy = nc.vector.tensor_copy
+        scopy = nc.scalar.copy
+        order = [(jt, b) for jt in range(TT) for b in range(B)]
 
         theta = const.tile([P, PAIRS], F32, name="theta")
         nc.vector.memset(theta[:, 0:1], 1.0)
         scratch = const.tile([P, 1], F32, name="scratch")
         nc.scalar.activation(out=scratch[:], in_=theta[:, 0:1], func=ACT.Sin)
-        ident = const.tile([P, P], F32, name="ident")
-        make_identity(nc, ident[:])
         t_int = const.tile([P, TT], I32, name="t_int")
         nc.gpsimd.iota(t_int[:], pattern=[[P, TT]], base=0, channel_multiplier=1)
+        ident = const.tile([P, P], F32, name="ident")
+        make_identity(nc, ident[:])
 
-        order = [(jt, b) for jt in range(TT) for b in range(B)]
-        x_raw = []
-        for n in range(NTILES):
-            x_raw.append(raw.tile([P, D], BF16, name="xr%d" % n))
+        x_raw = {}
         w_raw = {}
-        for w in range(2):
-            for k in range(2):
-                for m in range(4):
-                    w_raw[(w, k, m)] = raw.tile([P, D], BF16, name="wr%d_%d_%d" % (w, k, m))
 
         def load_x(n):
             jt, b = order[n]
-            nc.sync.dma_start(out=x_raw[n][:], in_=x[b, jt * P : (jt + 1) * P, :])
+            xr = raw.tile([P, D], BF16, name="xr")
+            nc.sync.dma_start(out=xr[:], in_=x[b, jt * P : (jt + 1) * P, :])
+            x_raw[n] = xr
 
         def load_w(w, k):
-            view = ws_dram[w].rearrange("(k mm q j) d -> k mm j q d", k=2, mm=2, q=P, j=2)
+            view = weights[w].rearrange("(k mm q j) d -> k mm j q d", k=2, mm=2, q=P, j=2)
             for m in range(4):
-                nc.sync.dma_start(out=w_raw[(w, k, m)][:], in_=view[k, m % 2, 1 - m // 2])
+                wr = raw.tile([P, D], BF16, name="wr")
+                nc.sync.dma_start(out=wr[:], in_=view[k, m % 2, 1 - m // 2])
+                w_raw[(w, k, m)] = wr
 
         load_x(0)
         load_w(0, 0)
         load_w(0, 1)
-        load_x(1)
-        load_w(1, 0)
-        load_w(1, 1)
-        for n in range(2, NTILES):
+        for n in range(1, RAW):
             load_x(n)
 
         n = 1
@@ -90,36 +94,48 @@ def tile_attention_pa_kernel(tc, x, wq, wk, out_0, out_1):
         nc.vector.tensor_scalar(out=t_turns[:], in0=t_int[:], scalar1=1.0 / (2 * math.pi), scalar2=None, op0=ALU.mult)
 
         table = const.tile([P, TT, 2, PAIRS, 2], F32, name="table")
+        wholes = {}
+        fracs = {}
+        trigs = {}
 
-        def make_table(jt, copier):
-            turns = stage.tile([P, PAIRS], F32, name="turns")
-            nc.vector.tensor_scalar(out=turns[:], in0=theta[:], scalar1=t_turns[:, jt : jt + 1], scalar2=None, op0=ALU.mult)
-            whole = stage.tile([P, PAIRS], I32, name="whole")
-            nc.vector.tensor_copy(out=whole[:], in_=turns[:])
-            frac = stage.tile([P, PAIRS], F32, name="frac")
-            nc.vector.tensor_tensor(out=frac[:], in0=turns[:], in1=whole[:], op=ALU.subtract)
-            trig = stage.tile([P, 3, PAIRS], F32, name="trig")
-            absf = stage.tile([P, PAIRS], F32, name="absf")
-            nc.scalar.activation(out=absf[:], in_=frac[:], func=ACT.Abs)
+        def table_whole(jt, engine):
+            whole = const.tile([P, PAIRS], I32, name="whole%d" % jt)
+            engine.tensor_scalar(out=whole[:], in0=theta[:], scalar1=t_turns[:, jt : jt + 1], scalar2=0.0, op0=ALU.mult, op1=ALU.add)
+            wholes[jt] = whole
+
+        def table_frac(jt):
+            frac = const.tile([P, PAIRS], F32, name="frac%d" % jt)
+            nc.vector.scalar_tensor_tensor(
+                out=frac[:], in0=theta[:], scalar=t_turns[:, jt : jt + 1], in1=wholes[jt][:], op0=ALU.mult, op1=ALU.subtract,
+            )
+            fracs[jt] = frac
+
+        def table_trig(jt):
+            trig = once.tile([P, 3, PAIRS], F32, name="trig")
+            absf = once.tile([P, PAIRS], F32, name="absf")
+            nc.scalar.activation(out=absf[:], in_=fracs[jt][:], func=ACT.Abs)
             nc.scalar.activation(out=trig[:, 1, :], in_=absf[:], func=ACT.Sin, scale=-2 * math.pi, bias=halfpi[:])
-            nc.scalar.activation(out=trig[:, 0, :], in_=frac[:], func=ACT.Sin, scale=-2 * math.pi)
-            nc.scalar.activation(out=trig[:, 2, :], in_=frac[:], func=ACT.Sin, scale=2 * math.pi)
-            for h in range(2):
-                copier(out=table[:, jt, h], in_=trig[:, h : h + 2, :].rearrange("p r i -> p i r"))
+            nc.scalar.activation(out=trig[:, 2, :], in_=fracs[jt][:], func=ACT.Sin, scale=2 * math.pi)
+            nc.scalar.activation(out=trig[:, 0, :], in_=fracs[jt][:], func=ACT.Sin, scale=-2 * math.pi)
+            trigs[jt] = trig
 
-        def turn(src, dst_words):
+        def table_weave(jt, copier):
+            for h in (1, 0):
+                copier(out=table[:, jt, h], in_=trigs[jt][:, h : h + 2, :].rearrange("p r i -> p i r"))
+
+        def turn(src, dst_words, copier):
             words = src[:].bitcast(F32)
             tp = tpp.tile([P, PASSES, 2, P], F32, name="tp")
             for g in range(PASSES):
                 for u in range(2):
                     nc.tensor.transpose(tp[:, g, u, :], words[:, 256 * g + u : 256 * (g + 1) : 2], ident[:])
-            nc.scalar.copy(out=dst_words, in_=tp[:].rearrange("p g u c -> p g c u"))
+            copier(out=dst_words, in_=tp[:].rearrange("p g u c -> p g c u"))
 
         x_codes = []
         x_scales = []
-        for n in range(NTILES):
-            x_codes.append(keep.tile([P, PASSES * P], U32, name="xc%d" % n, align_bytes=64))
-            x_scales.append(keep.tile([P, PASSES * P], U8, name="xs%d" % n, align_bytes=64))
+        for n in range(NTILES // 4):
+            x_codes.append(keep.tile([P, 4, PASSES * P], U32, name="xc%d" % n, align_bytes=64))
+            x_scales.append(keep.tile([P, 4, PASSES * P], U8, name="xs%d" % n, align_bytes=64))
         w_codes = {}
         w_scales = {}
         for w in range(2):
@@ -127,69 +143,151 @@ def tile_attention_pa_kernel(tc, x, wq, wk, out_0, out_1):
                 w_codes[(w, k)] = keep.tile([P, PASSES, BANK], U32, name="wc%d_%d" % (w, k), align_bytes=64)
                 w_scales[(w, k)] = keep.tile([P, PASSES, BANK], U8, name="ws%d_%d" % (w, k), align_bytes=64)
 
-        def prep_x(n):
-            gx = stage.tile([P, PASSES, P, 4], BF16, name="gx", align_bytes=64)
-            turn(x_raw[n], gx[:].bitcast(F32))
+        grouped_x = {}
+        grouped_w = {}
+
+        def turn_x(n, copier):
+            if n // 4 not in grouped_x:
+                gx = stage.tile([P, 4, PASSES, P, 4], BF16, name="gx", align_bytes=64)
+                grouped_x[n // 4] = gx
+            turn(x_raw[n], grouped_x[n // 4][:, n % 4].bitcast(F32), copier)
+            if n + RAW < NTILES:
+                load_x(n + RAW)
+
+        def turn_w(w, k, m, copier):
+            if (w, k) not in grouped_w:
+                gw = stage.tile([P, PASSES, BANK, 4], BF16, name="gw", align_bytes=64)
+                grouped_w[(w, k)] = gw
+            turn(w_raw[(w, k, m)], grouped_w[(w, k)][:].bitcast(F32)[:, :, m * P : (m + 1) * P, :], copier)
+
+        def quantize_x(first, count):
+            grp, lo = first // 4, first % 4
             nc.vector.quantize_mx(
-                out=x_codes[n][:].bitcast(FP8X4), scales=x_scales[n][:],
-                in_=gx[:].rearrange("p g c t -> p (g c t)"),
+                out=x_codes[grp][:, lo : lo + count].rearrange("p n c -> p (n c)").bitcast(FP8X4),
+                scales=x_scales[grp][:, lo : lo + count].rearrange("p n c -> p (n c)"),
+                in_=grouped_x[grp][:, lo : lo + count].rearrange("p n g c t -> p (n g c t)"),
             )
 
-        def prep_w(w, j):
-            gw = stage.tile([P, PASSES, BANK, 4], BF16, name="gw", align_bytes=64)
-            for m in range(4):
-                turn(w_raw[(w, j, m)], gw[:].bitcast(F32)[:, :, m * P : (m + 1) * P, :])
+        def quantize_w_half(w, k, half):
+            cols = slice(half * HALF, (half + 1) * HALF)
             for g in range(PASSES):
                 nc.vector.quantize_mx(
-                    out=w_codes[(w, j)][:, g, :].bitcast(FP8X4), scales=w_scales[(w, j)][:, g, :],
-                    in_=gw[:, g].rearrange("p c t -> p (c t)"),
+                    out=w_codes[(w, k)][:, g, cols].bitcast(FP8X4), scales=w_scales[(w, k)][:, g, cols],
+                    in_=grouped_w[(w, k)][:, g, cols, :].rearrange("p c t -> p (c t)"),
                 )
 
-        def project(n, w, j):
-            acc = accp.tile([P, BANK], F32, name="acc")
-            for g in range(PASSES):
-                cols = slice(g * P, (g + 1) * P)
-                nc.tensor.matmul_mx(
-                    out=acc[:],
-                    lhsT=x_codes[n][:, cols].bitcast(FP8X4), lhsT_scale=x_scales[n][:, cols],
-                    rhs=w_codes[(w, j)][:, g, :].bitcast(FP8X4), rhs_scale=w_scales[(w, j)][:, g, :],
-                    start=(g == 0), stop=(g == PASSES - 1),
-                )
-            return acc
+        def quantize_w(w, k):
+            nc.vector.quantize_mx(
+                out=w_codes[(w, k)][:].rearrange("p g c -> p (g c)").bitcast(FP8X4),
+                scales=w_scales[(w, k)][:].rearrange("p g c -> p (g c)"),
+                in_=grouped_w[(w, k)][:].rearrange("p g c t -> p (g c t)"),
+            )
 
-        def unit(n, w):
-            jt, b = order[n]
-            prod = work.tile([P, 2, 2, HALF, 2], F32, name="prod")
+        accs = {}
+
+        def project(unit):
+            n, w = unit
             for k in range(2):
-                acc = project(n, w, k)
+                acc = accp.tile([P, BANK], F32, name="acc")
+                for g in range(PASSES):
+                    cols = slice(g * P, (g + 1) * P)
+                    nc.tensor.matmul_mx(
+                        out=acc[:],
+                        lhsT=x_codes[n // 4][:, n % 4, cols].bitcast(FP8X4), lhsT_scale=x_scales[n // 4][:, n % 4, cols],
+                        rhs=w_codes[(w, k)][:, g, :].bitcast(FP8X4), rhs_scale=w_scales[(w, k)][:, g, :],
+                        start=(g == 0), stop=(g == PASSES - 1),
+                    )
+                accs[(n, w, k)] = acc
+
+        def multiply(unit, dst):
+            n, w = unit
+            for k in range(2):
                 nc.vector.tensor_tensor(
-                    out=prod[:, k],
-                    in0=acc[:].rearrange("p (h i) -> p h i", h=2).unsqueeze(3).to_broadcast([P, 2, HALF, 2]),
-                    in1=table[:, jt, :, k * HALF : (k + 1) * HALF, :],
+                    out=dst[:, k].rearrange("p h (i r) -> p h i r", r=2),
+                    in0=accs[(n, w, k)][:].rearrange("p (h i) -> p h i", h=2).unsqueeze(3).to_broadcast([P, 2, HALF, 2]),
+                    in1=table[:, order[n][0], :, k * HALF : (k + 1) * HALF, :],
                     op=ALU.mult,
                 )
-            rot = work.tile([P, 2, BANK], F32, name="rot")
-            halves = prod[:].rearrange("p k h i r -> p k h (i r)")
-            nc.gpsimd.tensor_tensor(out=rot[:], in0=halves[:, :, 0, :], in1=halves[:, :, 1, :], op=ALU.add)
-            nc.sync.dma_start(out=outs[w][b, jt * P : (jt + 1) * P, :], in_=rot[:].rearrange("p k e -> p (k e)"))
 
-        make_table(0, nc.vector.tensor_copy)
-        prep_x(0)
-        prep_w(0, 0)
-        prep_w(0, 1)
-        prep_x(1)
-        unit(0, 0)
-        prep_w(1, 0)
-        unit(1, 0)
-        prep_w(1, 1)
-        prep_x(2)
-        unit(0, 1)
-        prep_x(3)
-        unit(1, 1)
-        for n in range(2, NTILES):
-            if n + 2 < NTILES:
-                prep_x(n + 2)
-            if n % B == 2 and n // B + 1 < TT:
-                make_table(n // B + 1, nc.scalar.copy)
-            unit(n, 0)
-            unit(n, 1)
+        def add_store(members, lo, prod, rot, engine):
+            hi = lo + len(members)
+            engine.tensor_tensor(out=rot[:, lo:hi], in0=prod[:, lo:hi, :, 0, :], in1=prod[:, lo:hi, :, 1, :], op=ALU.add)
+            for i in range(len(members)):
+                n, w = members[i]
+                jt, b = order[n]
+                nc.sync.dma_start(out=outs[w][b, jt * P : (jt + 1) * P, :], in_=rot[:, lo + i].rearrange("p k e -> p (k e)"))
+
+        gate = const.tile([P, 1], U32, name="gate")
+
+        def hold_gpsimd(codes):
+            nc.gpsimd.tensor_copy(out=gate[:], in_=codes)
+
+        table_whole(0, nc.vector)
+        table_frac(0)
+        table_trig(0)
+        for jt in range(1, TT):
+            table_whole(jt, nc.gpsimd)
+        first_tiles = [(0, 0, m) for m in range(4)] + [(0, 1, m) for m in range(4)]
+        turn_x(0, vcopy)
+        for i in range(4):
+            turn_w(0, 0, i, vcopy if i + 1 < VECTOR_COPIES else scopy)
+        load_w(1, 0)
+        for jt in range(1, TT):
+            table_frac(jt)
+        quantize_x(0, 1)
+        quantize_w_half(0, 0, 0)
+        quantize_w_half(0, 0, 1)
+        for m in range(4):
+            turn_w(0, 1, m, scopy)
+        load_w(1, 1)
+        table_weave(0, vcopy)
+        quantize_w_half(0, 1, 0)
+        quantize_w_half(0, 1, 1)
+        for n in range(1, 4):
+            turn_x(n, scopy)
+        quantize_x(1, 1)
+        quantize_x(2, 2)
+        table_trig(1)
+        table_weave(1, scopy)
+
+        units = [(n, 0) for n in range(FIRST)] + [(n, 1) for n in range(FIRST)]
+        for n in range(FIRST, NTILES):
+            units.extend([(n, 0), (n, 1)])
+        ahead = [("x", n) for n in range(4, FIRST)]
+        ahead.extend([("w", k, m) for k in range(2) for m in range(4)])
+        ahead.extend([("x", n) for n in range(FIRST, NTILES)])
+        npairs = len(units) // 2
+        project(units[0])
+        for pair in range(npairs):
+            prod = work.tile([P, 2, 2, 2, BANK], F32, name="prod")
+            rot = work.tile([P, 2, 2, BANK], F32, name="rot", bufs=2)
+            split = pair == 0 or pair >= npairs - 2
+            for i in range(2):
+                u = 2 * pair + i
+                if u + 1 < len(units):
+                    project(units[u + 1])
+                for step in ahead[:TURNS_A_UNIT]:
+                    if step[0] == "x":
+                        turn_x(step[1], scopy)
+                    else:
+                        turn_w(1, step[1], step[2], scopy)
+                ahead = ahead[TURNS_A_UNIT:]
+                if u == 8 or u == 12:
+                    table_trig(u // 4)
+                    table_weave(u // 4, scopy)
+                multiply(units[u], prod[:, i])
+                if u == 1:
+                    quantize_x(4, 4)
+                    hold_gpsimd(x_codes[1][:, 3, 0:1])
+                if u == 5:
+                    quantize_w(1, 0)
+                    quantize_w(1, 1)
+                    hold_gpsimd(w_codes[(1, 1)][:, 1, 0:1])
+                if u == 9:
+                    quantize_x(8, 4)
+                    quantize_x(12, 4)
+                    hold_gpsimd(x_codes[3][:, 3, 0:1])
+                if split:
+                    add_store([units[u]], i, prod, rot, nc.vector if u == len(units) - 1 else nc.gpsimd)
+                elif i == 1:
+                    add_store([units[u - 1], units[u]], 0, prod, rot, nc.gpsimd)

@@ -227,7 +227,6 @@ def tile_attention_pa_kernel(tc, x, wq, wk, out_0, out_1):
         table_trig(0)
         for jt in range(1, TT):
             table_whole(jt, nc.gpsimd)
-        first_tiles = [(0, 0, m) for m in range(4)] + [(0, 1, m) for m in range(4)]
         turn_x(0, vcopy)
         for i in range(4):
             turn_w(0, 0, i, vcopy if i + 1 < VECTOR_COPIES else scopy)
@@ -287,7 +286,11 @@ def tile_attention_pa_kernel(tc, x, wq, wk, out_0, out_1):
                     quantize_x(8, 4)
                     quantize_x(12, 4)
                     hold_gpsimd(x_codes[3][:, 3, 0:1])
-                if split:
-                    add_store([units[u]], i, prod, rot, nc.vector if u == len(units) - 1 else nc.gpsimd)
+                if pair == npairs - 1:
+                    if i == 1:
+                        add_store([units[u - 1]], 0, prod, rot, nc.vector)
+                        add_store([units[u]], 1, prod, rot, nc.vector)
+                elif split:
+                    add_store([units[u]], i, prod, rot, nc.gpsimd)
                 elif i == 1:
                     add_store([units[u - 1], units[u]], 0, prod, rot, nc.gpsimd)

@@ -26,7 +26,7 @@ TT = S // P
 NTILES = B * TT
 RAW = 8
 FIRST = 8
-VECTOR_COPIES = 3
+VECTOR_COPIES = 4
 TURNS_A_UNIT = 3
 
 
@@ -93,10 +93,9 @@ def tile_attention_pa_kernel(tc, x, wq, wk, out_0, out_1):
         t_turns = const.tile([P, TT], F32, name="t_turns")
         nc.vector.tensor_scalar(out=t_turns[:], in0=t_int[:], scalar1=1.0 / (2 * math.pi), scalar2=None, op0=ALU.mult)
 
-        table = const.tile([P, TT, 2, PAIRS, 2], F32, name="table")
+        table = const.tile([P, TT, 2, 2, PAIRS], F32, name="table")
         wholes = {}
         fracs = {}
-        trigs = {}
 
         def table_whole(jt, engine):
             whole = const.tile([P, PAIRS], I32, name="whole%d" % jt)
@@ -111,17 +110,12 @@ def tile_attention_pa_kernel(tc, x, wq, wk, out_0, out_1):
             fracs[jt] = frac
 
         def table_trig(jt):
-            trig = once.tile([P, 3, PAIRS], F32, name="trig")
             absf = once.tile([P, PAIRS], F32, name="absf")
             nc.scalar.activation(out=absf[:], in_=fracs[jt][:], func=ACT.Abs)
-            nc.scalar.activation(out=trig[:, 1, :], in_=absf[:], func=ACT.Sin, scale=-2 * math.pi, bias=halfpi[:])
-            nc.scalar.activation(out=trig[:, 2, :], in_=fracs[jt][:], func=ACT.Sin, scale=2 * math.pi)
-            nc.scalar.activation(out=trig[:, 0, :], in_=fracs[jt][:], func=ACT.Sin, scale=-2 * math.pi)
-            trigs[jt] = trig
-
-        def table_weave(jt, copier):
-            for h in (1, 0):
-                copier(out=table[:, jt, h], in_=trigs[jt][:, h : h + 2, :].rearrange("p r i -> p i r"))
+            nc.scalar.activation(out=table[:, jt, 1, 1, :], in_=fracs[jt][:], func=ACT.Sin, scale=2 * math.pi)
+            nc.scalar.activation(out=table[:, jt, 0, 0, :], in_=fracs[jt][:], func=ACT.Sin, scale=-2 * math.pi)
+            for h in range(2):
+                nc.scalar.activation(out=table[:, jt, h, 1 - h, :], in_=absf[:], func=ACT.Sin, scale=-2 * math.pi, bias=halfpi[:])
 
         def turn(src, dst_words, copier):
             words = src[:].bitcast(F32)
@@ -205,7 +199,7 @@ def tile_attention_pa_kernel(tc, x, wq, wk, out_0, out_1):
                 nc.vector.tensor_tensor(
                     out=dst[:, k].rearrange("p h (i r) -> p h i r", r=2),
                     in0=accs[(n, w, k)][:].rearrange("p (h i) -> p h i", h=2).unsqueeze(3).to_broadcast([P, 2, HALF, 2]),
-                    in1=table[:, order[n][0], :, k * HALF : (k + 1) * HALF, :],
+                    in1=table[:, order[n][0], :, :, k * HALF : (k + 1) * HALF].rearrange("p h r i -> p h i r"),
                     op=ALU.mult,
                 )
 
@@ -239,7 +233,6 @@ def tile_attention_pa_kernel(tc, x, wq, wk, out_0, out_1):
         for m in range(4):
             turn_w(0, 1, m, scopy)
         load_w(1, 1)
-        table_weave(0, vcopy)
         quantize_w_half(0, 1, 0)
         quantize_w_half(0, 1, 1)
         for n in range(1, 4):
@@ -247,7 +240,6 @@ def tile_attention_pa_kernel(tc, x, wq, wk, out_0, out_1):
         quantize_x(1, 1)
         quantize_x(2, 2)
         table_trig(1)
-        table_weave(1, scopy)
 
         units = [(n, 0) for n in range(FIRST)] + [(n, 1) for n in range(FIRST)]
         for n in range(FIRST, NTILES):
@@ -273,7 +265,6 @@ def tile_attention_pa_kernel(tc, x, wq, wk, out_0, out_1):
                 ahead = ahead[TURNS_A_UNIT:]
                 if u == 8 or u == 12:
                     table_trig(u // 4)
-                    table_weave(u // 4, scopy)
                 multiply(units[u], prod[:, i])
                 if u == 1:
                     quantize_x(4, 4)

@@ -28,6 +28,16 @@ RAW = 8
 FIRST = 8
 VECTOR_COPIES = 4
 TURNS_A_UNIT = 3
+M_SIN, COS, SIN, GA, GB = 0, 1, 2, 3, 4
+GAUSS_FROM = 4
+PLAIN_EVERY = 4
+VADD_FROM = 20
+VADD_EVERY = 20
+VRED_EVERY = 2
+VRED_PHASE = 1
+JOBS_FROM = 2
+ROTS = 3
+PRODS = 3
 
 
 def tile_attention_pa_kernel(tc, x, wq, wk, out_0, out_1):
@@ -42,8 +52,7 @@ def tile_attention_pa_kernel(tc, x, wq, wk, out_0, out_1):
         stage = ctx.enter_context(tc.tile_pool(name="stage", bufs=2))
         once = ctx.enter_context(tc.tile_pool(name="once", bufs=1))
         work = ctx.enter_context(tc.tile_pool(name="work", bufs=3))
-        tpp = ctx.enter_context(tc.psum_pool(name="tpp", bufs=4))
-        accp = ctx.enter_context(tc.psum_pool(name="accp", bufs=4))
+        banks = ctx.enter_context(tc.psum_pool(name="banks", bufs=8))
         ctx.enter_context(tc.manual_schedule())
 
         vcopy = nc.vector.tensor_copy
@@ -69,10 +78,10 @@ def tile_attention_pa_kernel(tc, x, wq, wk, out_0, out_1):
             x_raw[n] = xr
 
         def load_w(w, k):
-            view = weights[w].rearrange("(k mm q j) d -> k mm j q d", k=2, mm=2, q=P, j=2)
+            view = weights[w].rearrange("(m q j) d -> m j q d", m=4, q=P, j=2)
             for m in range(4):
                 wr = raw.tile([P, D], BF16, name="wr")
-                nc.sync.dma_start(out=wr[:], in_=view[k, m % 2, 1 - m // 2])
+                nc.sync.dma_start(out=wr[:], in_=view[m, 1 - k])
                 w_raw[(w, k, m)] = wr
 
         load_x(0)
@@ -90,10 +99,13 @@ def tile_attention_pa_kernel(tc, x, wq, wk, out_0, out_1):
             n *= 2
         halfpi = const.tile([P, 1], F32, name="halfpi")
         nc.vector.tensor_scalar(out=halfpi[:], in0=theta[:, 0:1], scalar1=math.pi / 2, scalar2=None, op0=ALU.mult)
+        shifts = const.tile([P, 3], F32, name="shifts")
+        for col, value in enumerate((-math.pi / 4, math.pi / 4, -math.pi / 2)):
+            nc.vector.tensor_scalar(out=shifts[:, col : col + 1], in0=theta[:, 0:1], scalar1=value, scalar2=None, op0=ALU.mult)
         t_turns = const.tile([P, TT], F32, name="t_turns")
         nc.vector.tensor_scalar(out=t_turns[:], in0=t_int[:], scalar1=1.0 / (2 * math.pi), scalar2=None, op0=ALU.mult)
 
-        table = const.tile([P, TT, 2, 2, PAIRS], F32, name="table")
+        table = const.tile([P, TT, 5, PAIRS], F32, name="table")
         wholes = {}
         fracs = {}
 
@@ -110,16 +122,27 @@ def tile_attention_pa_kernel(tc, x, wq, wk, out_0, out_1):
             fracs[jt] = frac
 
         def table_trig(jt):
+            nc.scalar.activation(out=table[:, jt, M_SIN, :], in_=fracs[jt][:], func=ACT.Sin, scale=-2 * math.pi)
+            table_cos(jt)
+            nc.scalar.activation(out=table[:, jt, SIN, :], in_=fracs[jt][:], func=ACT.Sin, scale=2 * math.pi)
+
+        def table_sines(jt):
+            nc.scalar.activation(out=table[:, jt, M_SIN, :], in_=fracs[jt][:], func=ACT.Sin, scale=-2 * math.pi)
+            nc.scalar.activation(out=table[:, jt, SIN, :], in_=fracs[jt][:], func=ACT.Sin, scale=2 * math.pi)
+
+        def table_cos(jt):
             absf = once.tile([P, PAIRS], F32, name="absf")
             nc.scalar.activation(out=absf[:], in_=fracs[jt][:], func=ACT.Abs)
-            nc.scalar.activation(out=table[:, jt, 1, 1, :], in_=fracs[jt][:], func=ACT.Sin, scale=2 * math.pi)
-            nc.scalar.activation(out=table[:, jt, 0, 0, :], in_=fracs[jt][:], func=ACT.Sin, scale=-2 * math.pi)
-            for h in range(2):
-                nc.scalar.activation(out=table[:, jt, h, 1 - h, :], in_=absf[:], func=ACT.Sin, scale=-2 * math.pi, bias=halfpi[:])
+            nc.scalar.activation(out=table[:, jt, COS, :], in_=absf[:], func=ACT.Sin, scale=-2 * math.pi, bias=halfpi[:])
+
+        def table_gauss(jt, h):
+            absf = once.tile([P, PAIRS], F32, name="absf")
+            nc.scalar.activation(out=absf[:], in_=fracs[jt][:], func=ACT.Abs, scale=2 * math.pi, bias=shifts[:, h : h + 1])
+            nc.scalar.activation(out=table[:, jt, GA + h, :], in_=absf[:], func=ACT.Sin, bias=shifts[:, 2:3])
 
         def turn(src, dst_words, copier):
             words = src[:].bitcast(F32)
-            tp = tpp.tile([P, PASSES, 2, P], F32, name="tp")
+            tp = banks.tile([P, PASSES, 2, P], F32, name="bank")
             for g in range(PASSES):
                 for u in range(2):
                     nc.tensor.transpose(tp[:, g, u, :], words[:, 256 * g + u : 256 * (g + 1) : 2], ident[:])
@@ -179,37 +202,81 @@ def tile_attention_pa_kernel(tc, x, wq, wk, out_0, out_1):
 
         accs = {}
 
-        def project(unit):
+        def project(unit, gauss):
             n, w = unit
-            for k in range(2):
-                acc = accp.tile([P, BANK], F32, name="acc")
-                for g in range(PASSES):
+            groups = [[0], [1], [0, 1]] if gauss else [[0], [1]]
+            for k, parts in enumerate(groups):
+                acc = banks.tile([P, BANK], F32, name="bank")
+                steps = [(g, part) for g in range(PASSES) for part in parts]
+                for j, (g, part) in enumerate(steps):
                     cols = slice(g * P, (g + 1) * P)
                     nc.tensor.matmul_mx(
                         out=acc[:],
                         lhsT=x_codes[n // 4][:, n % 4, cols].bitcast(FP8X4), lhsT_scale=x_scales[n // 4][:, n % 4, cols],
-                        rhs=w_codes[(w, k)][:, g, :].bitcast(FP8X4), rhs_scale=w_scales[(w, k)][:, g, :],
-                        start=(g == 0), stop=(g == PASSES - 1),
+                        rhs=w_codes[(w, part)][:, g, :].bitcast(FP8X4), rhs_scale=w_scales[(w, part)][:, g, :],
+                        start=(j == 0), stop=(j == len(steps) - 1),
                     )
                 accs[(n, w, k)] = acc
 
-        def multiply(unit, dst):
+        def multiply(unit, dst, gauss):
             n, w = unit
+            jt = order[n][0]
             for k in range(2):
-                nc.vector.tensor_tensor(
-                    out=dst[:, k].rearrange("p h (i r) -> p h i r", r=2),
-                    in0=accs[(n, w, k)][:].rearrange("p (h i) -> p h i", h=2).unsqueeze(3).to_broadcast([P, 2, HALF, 2]),
-                    in1=table[:, order[n][0], :, :, k * HALF : (k + 1) * HALF].rearrange("p h r i -> p h i r"),
-                    op=ALU.mult,
-                )
+                if gauss:
+                    nc.vector.scalar_tensor_tensor(
+                        out=dst[:, 0, k * PAIRS : (k + 1) * PAIRS], in0=accs[(n, w, k)][:], scalar=math.sqrt(2.0),
+                        in1=table[:, jt, GA + k, :], op0=ALU.mult, op1=ALU.mult,
+                    )
+                else:
+                    nc.vector.tensor_tensor(
+                        out=dst[:, k].rearrange("p (i r) -> p i r", r=2),
+                        in0=accs[(n, w, k)][:].unsqueeze(2).to_broadcast([P, PAIRS, 2]),
+                        in1=table[:, jt, k : k + 2, :].rearrange("p r i -> p i r"),
+                        op=ALU.mult,
+                    )
+            if gauss:
+                nc.vector.tensor_tensor(out=dst[:, 1, 0:PAIRS], in0=accs[(n, w, 2)][:], in1=table[:, jt, COS, :], op=ALU.mult)
 
-        def add_store(members, lo, prod, rot, engine):
-            hi = lo + len(members)
-            engine.tensor_tensor(out=rot[:, lo:hi], in0=prod[:, lo:hi, :, 0, :], in1=prod[:, lo:hi, :, 1, :], op=ALU.add)
-            for i in range(len(members)):
-                n, w = members[i]
+        def add(members, lo, prod, rot, on_vector, gauss, reduce=False):
+            count = len(members)
+            hi = lo + count
+            engine = nc.vector if on_vector else nc.gpsimd
+            if not gauss:
+                engine.tensor_tensor(out=rot[:, lo:hi], in0=prod[:, lo:hi, 0, :], in1=prod[:, lo:hi, 1, :], op=ALU.add)
+            elif on_vector:
+                for i in range(lo, hi):
+                    engine.tensor_tensor(
+                        out=rot[:, i].rearrange("p (i r) -> p i r", r=2),
+                        in0=prod[:, i, 0, :].rearrange("p (r i) -> p i r", r=2),
+                        in1=prod[:, i, 1, 0:PAIRS].unsqueeze(2).to_broadcast([P, PAIRS, 2]),
+                        op=ALU.add,
+                    )
+            elif reduce:
+                for i in range(lo, hi):
+                    flat = prod[:, i].rearrange("p k e -> p (k e)")
+                    for r in (1, 0):
+                        nc.vector.tensor_reduce(
+                            out=flat[:, (2 * r + 1) * PAIRS : (2 * r + 2) * PAIRS],
+                            in_=flat[:, r * PAIRS : 2 * E - r * PAIRS].rearrange("p (j e) -> p e j", j=2)[:, 0:PAIRS, :],
+                            axis=mybir.AxisListType.X, op=ALU.add,
+                        )
+            else:
+                own = prod[:, lo:hi, 0, :].rearrange("p u (r i) -> p u r i", r=2)
+                engine.tensor_tensor(
+                    out=own, in0=own, in1=prod[:, lo:hi, 1, 0:PAIRS].unsqueeze(2).to_broadcast([P, count, 2, PAIRS]), op=ALU.add,
+                )
+            weave = 0 if on_vector or not gauss else (2 if reduce else 1)
+            return [(members[i], lo + i, prod, rot, weave) for i in range(count)]
+
+        def finish(steps):
+            for (n, w), slot, prod, rot, weave in steps:
+                if weave == 1:
+                    scopy(out=rot[:, slot].rearrange("p (i r) -> p i r", r=2), in_=prod[:, slot, 0, :].rearrange("p (r i) -> p i r", r=2))
+                if weave == 2:
+                    quarters = prod[:, slot].rearrange("p k (q i) -> p i (k q)", q=2)
+                    scopy(out=rot[:, slot].rearrange("p (i r) -> p i r", r=2), in_=quarters[:, :, 1::2])
                 jt, b = order[n]
-                nc.sync.dma_start(out=outs[w][b, jt * P : (jt + 1) * P, :], in_=rot[:, lo + i].rearrange("p k e -> p (k e)"))
+                nc.sync.dma_start(out=outs[w][b, jt * P : (jt + 1) * P, :], in_=rot[:, slot])
 
         gate = const.tile([P, 1], U32, name="gate")
 
@@ -248,24 +315,45 @@ def tile_attention_pa_kernel(tc, x, wq, wk, out_0, out_1):
         ahead.extend([("w", k, m) for k in range(2) for m in range(4)])
         ahead.extend([("x", n) for n in range(FIRST, NTILES)])
         npairs = len(units) // 2
-        project(units[0])
+
+        def is_gauss(pair):
+            return pair >= GAUSS_FROM and (PLAIN_EVERY == 0 or (pair - GAUSS_FROM) % PLAIN_EVERY != PLAIN_EVERY - 1)
+
+        def on_vector(pair):
+            return pair == npairs - 1 or (pair >= VADD_FROM and (pair - VADD_FROM) % VADD_EVERY == 0)
+
+        jobs = []
+        for jt in range(TT):
+            users = [pair for pair in range(npairs) if order[units[2 * pair][0]][0] == jt]
+            if jt >= 2:
+                jobs.append((table_cos, (jt,)))
+            if any(is_gauss(pair) for pair in users):
+                jobs.extend([(table_gauss, (jt, 0)), (table_gauss, (jt, 1))])
+            if jt >= 2 and not all(is_gauss(pair) for pair in users):
+                jobs.append((table_sines, (jt,)))
+        waiting = []
+
+        project(units[0], is_gauss(0))
         for pair in range(npairs):
-            prod = work.tile([P, 2, 2, 2, BANK], F32, name="prod")
-            rot = work.tile([P, 2, 2, BANK], F32, name="rot", bufs=2)
+            prod = work.tile([P, 2, 2, E], F32, name="prod", bufs=PRODS)
+            rot = work.tile([P, 2, E], F32, name="rot", bufs=ROTS)
             split = pair == 0 or pair >= npairs - 2
+            gauss = is_gauss(pair)
             for i in range(2):
                 u = 2 * pair + i
                 if u + 1 < len(units):
-                    project(units[u + 1])
+                    project(units[u + 1], is_gauss((u + 1) // 2))
                 for step in ahead[:TURNS_A_UNIT]:
                     if step[0] == "x":
                         turn_x(step[1], scopy)
                     else:
                         turn_w(1, step[1], step[2], scopy)
                 ahead = ahead[TURNS_A_UNIT:]
-                if u == 8 or u == 12:
-                    table_trig(u // 4)
-                multiply(units[u], prod[:, i])
+                if u >= JOBS_FROM and jobs:
+                    make, args = jobs[0]
+                    make(*args)
+                    jobs = jobs[1:]
+                multiply(units[u], prod[:, i], gauss)
                 if u == 1:
                     quantize_x(4, 4)
                     hold_gpsimd(x_codes[1][:, 3, 0:1])
@@ -279,9 +367,19 @@ def tile_attention_pa_kernel(tc, x, wq, wk, out_0, out_1):
                     hold_gpsimd(x_codes[3][:, 3, 0:1])
                 if pair == npairs - 1:
                     if i == 1:
-                        add_store([units[u - 1]], 0, prod, rot, nc.vector)
-                        add_store([units[u]], 1, prod, rot, nc.vector)
-                elif split:
-                    add_store([units[u]], i, prod, rot, nc.gpsimd)
-                elif i == 1:
-                    add_store([units[u - 1], units[u]], 0, prod, rot, nc.gpsimd)
+                        finish(waiting)
+                        finish(add([units[u - 1]], 0, prod, rot, True, gauss))
+                        finish(add([units[u]], 1, prod, rot, True, gauss))
+                elif split or i == 1:
+                    if split:
+                        steps = add([units[u]], i, prod, rot, on_vector(pair), gauss)
+                    elif gauss and not on_vector(pair) and VRED_EVERY > 0 and pair % VRED_EVERY == VRED_PHASE:
+                        steps = add([units[u - 1]], 0, prod, rot, False, gauss, True) + add([units[u]], 1, prod, rot, False, gauss)
+                    else:
+                        steps = add([units[u - 1], units[u]], 0, prod, rot, on_vector(pair), gauss)
+                    finish(waiting)
+                    waiting = []
+                    if gauss and not on_vector(pair):
+                        waiting = steps
+                    else:
+                        finish(steps)

@@ -30,14 +30,15 @@ VECTOR_COPIES = 4
 TURNS_A_UNIT = 3
 M_SIN, COS, SIN, GA, GB = 0, 1, 2, 3, 4
 GAUSS_FROM = 4
-PLAIN_EVERY = 4
+PLAIN_EVERY = 0
 VADD_FROM = 20
 VADD_EVERY = 20
-VRED_EVERY = 2
-VRED_PHASE = 1
+VRED_EVERY = 5
+VRED_PHASE = 3
 JOBS_FROM = 2
-ROTS = 3
-PRODS = 3
+FULL_TABLES = 2
+ROTS = 2
+PRODS = 4
 
 
 def tile_attention_pa_kernel(tc, x, wq, wk, out_0, out_1):
@@ -105,7 +106,13 @@ def tile_attention_pa_kernel(tc, x, wq, wk, out_0, out_1):
         t_turns = const.tile([P, TT], F32, name="t_turns")
         nc.vector.tensor_scalar(out=t_turns[:], in0=t_int[:], scalar1=1.0 / (2 * math.pi), scalar2=None, op0=ALU.mult)
 
-        table = const.tile([P, TT, 5, PAIRS], F32, name="table")
+        table = const.tile([P, FULL_TABLES, 5, PAIRS], F32, name="table")
+        lean = const.tile([P, TT - FULL_TABLES, 3, PAIRS], F32, name="lean")
+
+        def plane(jt, which):
+            if jt < FULL_TABLES:
+                return table[:, jt, which, :]
+            return lean[:, jt - FULL_TABLES, (COS, GA, GB).index(which), :]
         wholes = {}
         fracs = {}
 
@@ -133,12 +140,12 @@ def tile_attention_pa_kernel(tc, x, wq, wk, out_0, out_1):
         def table_cos(jt):
             absf = once.tile([P, PAIRS], F32, name="absf")
             nc.scalar.activation(out=absf[:], in_=fracs[jt][:], func=ACT.Abs)
-            nc.scalar.activation(out=table[:, jt, COS, :], in_=absf[:], func=ACT.Sin, scale=-2 * math.pi, bias=halfpi[:])
+            nc.scalar.activation(out=plane(jt, COS), in_=absf[:], func=ACT.Sin, scale=-2 * math.pi, bias=halfpi[:])
 
         def table_gauss(jt, h):
             absf = once.tile([P, PAIRS], F32, name="absf")
             nc.scalar.activation(out=absf[:], in_=fracs[jt][:], func=ACT.Abs, scale=2 * math.pi, bias=shifts[:, h : h + 1])
-            nc.scalar.activation(out=table[:, jt, GA + h, :], in_=absf[:], func=ACT.Sin, bias=shifts[:, 2:3])
+            nc.scalar.activation(out=plane(jt, GA + h), in_=absf[:], func=ACT.Sin, bias=shifts[:, 2:3])
 
         def turn(src, dst_words, copier):
             words = src[:].bitcast(F32)
@@ -225,7 +232,7 @@ def tile_attention_pa_kernel(tc, x, wq, wk, out_0, out_1):
                 if gauss:
                     nc.vector.scalar_tensor_tensor(
                         out=dst[:, 0, k * PAIRS : (k + 1) * PAIRS], in0=accs[(n, w, k)][:], scalar=math.sqrt(2.0),
-                        in1=table[:, jt, GA + k, :], op0=ALU.mult, op1=ALU.mult,
+                        in1=plane(jt, GA + k), op0=ALU.mult, op1=ALU.mult,
                     )
                 else:
                     nc.vector.tensor_tensor(
@@ -235,7 +242,7 @@ def tile_attention_pa_kernel(tc, x, wq, wk, out_0, out_1):
                         op=ALU.mult,
                     )
             if gauss:
-                nc.vector.tensor_tensor(out=dst[:, 1, 0:PAIRS], in0=accs[(n, w, 2)][:], in1=table[:, jt, COS, :], op=ALU.mult)
+                nc.vector.tensor_tensor(out=dst[:, 1, 0:PAIRS], in0=accs[(n, w, 2)][:], in1=plane(jt, COS), op=ALU.mult)
 
         def add(members, lo, prod, rot, on_vector, gauss, reduce=False):
             count = len(members)

@@ -27,7 +27,7 @@ NTILES = B * TT
 RAW = 8
 FIRST = 8
 VECTOR_COPIES = 4
-TURNS_A_UNIT = 3
+TURNS_A_UNIT = 4
 M_SIN, COS, SIN, GA, GB = 0, 1, 2, 3, 4
 GAUSS_FROM = 4
 PLAIN_EVERY = 0
@@ -37,7 +37,7 @@ VRED_EVERY = 5
 VRED_PHASE = 3
 JOBS_FROM = 2
 FULL_TABLES = 2
-ROTS = 2
+ROTS = 3
 PRODS = 4
 
 
@@ -117,7 +117,7 @@ def tile_attention_pa_kernel(tc, x, wq, wk, out_0, out_1):
         fracs = {}
 
         def table_whole(jt, engine):
-            whole = const.tile([P, PAIRS], I32, name="whole%d" % jt)
+            whole = work.tile([P, PAIRS], I32, name="rot", bufs=ROTS)
             engine.tensor_scalar(out=whole[:], in0=theta[:], scalar1=t_turns[:, jt : jt + 1], scalar2=0.0, op0=ALU.mult, op1=ALU.add)
             wholes[jt] = whole
 
@@ -374,9 +374,9 @@ def tile_attention_pa_kernel(tc, x, wq, wk, out_0, out_1):
                     hold_gpsimd(x_codes[3][:, 3, 0:1])
                 if pair == npairs - 1:
                     if i == 1:
-                        finish(waiting)
                         finish(add([units[u - 1]], 0, prod, rot, True, gauss))
                         finish(add([units[u]], 1, prod, rot, True, gauss))
+                        finish(waiting)
                 elif split or i == 1:
                     if split:
                         steps = add([units[u]], i, prod, rot, on_vector(pair), gauss)

@@ -30,7 +30,7 @@ VECTOR_COPIES = 4
 TURNS_A_UNIT = 4
 M_SIN, COS, SIN, GA, GB = 0, 1, 2, 3, 4
 GAUSS_FROM = 4
-PLAIN_EVERY = 0
+PLAIN_PAIRS = (7,)
 VADD_FROM = 20
 VADD_EVERY = 20
 VRED_EVERY = 5
@@ -324,7 +324,7 @@ def tile_attention_pa_kernel(tc, x, wq, wk, out_0, out_1):
         npairs = len(units) // 2
 
         def is_gauss(pair):
-            return pair >= GAUSS_FROM and (PLAIN_EVERY == 0 or (pair - GAUSS_FROM) % PLAIN_EVERY != PLAIN_EVERY - 1)
+            return pair >= GAUSS_FROM and pair not in PLAIN_PAIRS
 
         def on_vector(pair):
             return pair == npairs - 1 or (pair >= VADD_FROM and (pair - VADD_FROM) % VADD_EVERY == 0)

@@ -27,7 +27,7 @@ NTILES = B * TT
 RAW = 8
 FIRST = 8
 VECTOR_COPIES = 4
-TURNS_A_UNIT = 4
+TURNS_A_UNIT = 3
 M_SIN, COS, SIN, GA, GB = 0, 1, 2, 3, 4
 GAUSS_FROM = 4
 PLAIN_PAIRS = (7,)

@@ -24,19 +24,19 @@ BANK = 512
 HALF = BANK // 2
 TT = S // P
 NTILES = B * TT
-RAW = 8
+RAW = 7
 FIRST = 8
 VECTOR_COPIES = 4
 TURNS_A_UNIT = 3
 M_SIN, COS, SIN, GA, GB = 0, 1, 2, 3, 4
 GAUSS_FROM = 4
-PLAIN_PAIRS = (7,)
+PLAIN_PAIRS = (14,)
 VADD_FROM = 20
 VADD_EVERY = 20
 VRED_EVERY = 5
 VRED_PHASE = 3
 JOBS_FROM = 2
-FULL_TABLES = 2
+FULL_TABLES = (0, 1, 3)
 ROTS = 3
 PRODS = 4
 
@@ -106,13 +106,14 @@ def tile_attention_pa_kernel(tc, x, wq, wk, out_0, out_1):
         t_turns = const.tile([P, TT], F32, name="t_turns")
         nc.vector.tensor_scalar(out=t_turns[:], in0=t_int[:], scalar1=1.0 / (2 * math.pi), scalar2=None, op0=ALU.mult)
 
-        table = const.tile([P, FULL_TABLES, 5, PAIRS], F32, name="table")
-        lean = const.tile([P, TT - FULL_TABLES, 3, PAIRS], F32, name="lean")
+        table = const.tile([P, len(FULL_TABLES), 5, PAIRS], F32, name="table")
+        lean = const.tile([P, TT - len(FULL_TABLES), 3, PAIRS], F32, name="lean")
+        lean_tables = [jt for jt in range(TT) if jt not in FULL_TABLES]
 
         def plane(jt, which):
-            if jt < FULL_TABLES:
-                return table[:, jt, which, :]
-            return lean[:, jt - FULL_TABLES, (COS, GA, GB).index(which), :]
+            if jt in FULL_TABLES:
+                return table[:, FULL_TABLES.index(jt), which, :]
+            return lean[:, lean_tables.index(jt), (COS, GA, GB).index(which), :]
         wholes = {}
         fracs = {}
 
@@ -129,13 +130,13 @@ def tile_attention_pa_kernel(tc, x, wq, wk, out_0, out_1):
             fracs[jt] = frac
 
         def table_trig(jt):
-            nc.scalar.activation(out=table[:, jt, M_SIN, :], in_=fracs[jt][:], func=ACT.Sin, scale=-2 * math.pi)
+            nc.scalar.activation(out=plane(jt, M_SIN), in_=fracs[jt][:], func=ACT.Sin, scale=-2 * math.pi)
             table_cos(jt)
-            nc.scalar.activation(out=table[:, jt, SIN, :], in_=fracs[jt][:], func=ACT.Sin, scale=2 * math.pi)
+            nc.scalar.activation(out=plane(jt, SIN), in_=fracs[jt][:], func=ACT.Sin, scale=2 * math.pi)
 
         def table_sines(jt):
-            nc.scalar.activation(out=table[:, jt, M_SIN, :], in_=fracs[jt][:], func=ACT.Sin, scale=-2 * math.pi)
-            nc.scalar.activation(out=table[:, jt, SIN, :], in_=fracs[jt][:], func=ACT.Sin, scale=2 * math.pi)
+            nc.scalar.activation(out=plane(jt, M_SIN), in_=fracs[jt][:], func=ACT.Sin, scale=-2 * math.pi)
+            nc.scalar.activation(out=plane(jt, SIN), in_=fracs[jt][:], func=ACT.Sin, scale=2 * math.pi)
 
         def table_cos(jt):
             absf = once.tile([P, PAIRS], F32, name="absf")
@@ -238,7 +239,7 @@ def tile_attention_pa_kernel(tc, x, wq, wk, out_0, out_1):
                     nc.vector.tensor_tensor(
                         out=dst[:, k].rearrange("p (i r) -> p i r", r=2),
                         in0=accs[(n, w, k)][:].unsqueeze(2).to_broadcast([P, PAIRS, 2]),
-                        in1=table[:, jt, k : k + 2, :].rearrange("p r i -> p i r"),
+                        in1=table[:, FULL_TABLES.index(jt), k : k + 2, :].rearrange("p r i -> p i r"),
                         op=ALU.mult,
                     )
             if gauss:

@@ -24,13 +24,13 @@ BANK = 512
 HALF = BANK // 2
 TT = S // P
 NTILES = B * TT
-RAW = 7
+RAW = 8
 FIRST = 8
 VECTOR_COPIES = 4
 TURNS_A_UNIT = 3
 M_SIN, COS, SIN, GA, GB = 0, 1, 2, 3, 4
 GAUSS_FROM = 4
-PLAIN_PAIRS = (14,)
+PLAIN_PAIRS = (7, 14)
 VADD_FROM = 20
 VADD_EVERY = 20
 VRED_EVERY = 5
@@ -60,7 +60,7 @@ def tile_attention_pa_kernel(tc, x, wq, wk, out_0, out_1):
         scopy = nc.scalar.copy
         order = [(jt, b) for jt in range(TT) for b in range(B)]
 
-        theta = const.tile([P, PAIRS], F32, name="theta")
+        theta = work.tile([P, PAIRS], F32, name="prod", bufs=PRODS)
         nc.vector.memset(theta[:, 0:1], 1.0)
         scratch = const.tile([P, 1], F32, name="scratch")
         nc.scalar.activation(out=scratch[:], in_=theta[:, 0:1], func=ACT.Sin)

@@ -26,7 +26,7 @@ TT = S // P
 NTILES = B * TT
 RAW = 8
 FIRST = 8
-VECTOR_COPIES = 4
+VECTOR_COPIES = 5
 TURNS_A_UNIT = 3
 M_SIN, COS, SIN, GA, GB = 0, 1, 2, 3, 4
 GAUSS_FROM = 4
@@ -117,22 +117,36 @@ def tile_attention_pa_kernel(tc, x, wq, wk, out_0, out_1):
         wholes = {}
         fracs = {}
 
+        def wound(jt):
+            first_small = PAIRS * math.log10((P * (jt + 1) - 1) / math.pi) / math.log10(THETA)
+            return 8 * (int(first_small) // 8 + 1)
+
         def table_whole(jt, engine):
             whole = work.tile([P, PAIRS], I32, name="rot", bufs=ROTS)
-            engine.tensor_scalar(out=whole[:], in0=theta[:], scalar1=t_turns[:, jt : jt + 1], scalar2=0.0, op0=ALU.mult, op1=ALU.add)
+            n = wound(jt)
+            engine.tensor_scalar(out=whole[:, 0:n], in0=theta[:, 0:n], scalar1=t_turns[:, jt : jt + 1], scalar2=0.0, op0=ALU.mult, op1=ALU.add)
             wholes[jt] = whole
 
-        def table_frac(jt):
+        def table_small(jt):
             frac = const.tile([P, PAIRS], F32, name="frac%d" % jt)
-            nc.vector.scalar_tensor_tensor(
-                out=frac[:], in0=theta[:], scalar=t_turns[:, jt : jt + 1], in1=wholes[jt][:], op0=ALU.mult, op1=ALU.subtract,
-            )
+            n = wound(jt)
+            nc.gpsimd.tensor_scalar(out=frac[:, n:PAIRS], in0=theta[:, n:PAIRS], scalar1=t_turns[:, jt : jt + 1], scalar2=0.0, op0=ALU.mult, op1=ALU.add)
             fracs[jt] = frac
+
+        def table_frac(jt):
+            n = wound(jt)
+            nc.vector.scalar_tensor_tensor(
+                out=fracs[jt][:, 0:n], in0=theta[:, 0:n], scalar=t_turns[:, jt : jt + 1], in1=wholes[jt][:, 0:n], op0=ALU.mult, op1=ALU.subtract,
+            )
 
         def table_trig(jt):
             nc.scalar.activation(out=plane(jt, M_SIN), in_=fracs[jt][:], func=ACT.Sin, scale=-2 * math.pi)
             table_cos(jt)
             nc.scalar.activation(out=plane(jt, SIN), in_=fracs[jt][:], func=ACT.Sin, scale=2 * math.pi)
+
+        def table_first():
+            nc.scalar.activation(out=plane(0, SIN), in_=fracs[0][:], func=ACT.Sin, scale=2 * math.pi)
+            table_cos(0)
 
         def table_sines(jt):
             nc.scalar.activation(out=plane(jt, M_SIN), in_=fracs[jt][:], func=ACT.Sin, scale=-2 * math.pi)
@@ -226,6 +240,17 @@ def tile_attention_pa_kernel(tc, x, wq, wk, out_0, out_1):
                     )
                 accs[(n, w, k)] = acc
 
+        def multiply_part(unit, dst, lo, hi):
+            n, w = unit
+            jt = order[n][0]
+            for k in range(2):
+                nc.vector.tensor_tensor(
+                    out=dst[:, k, 2 * lo : 2 * hi].rearrange("p (i r) -> p i r", r=2),
+                    in0=accs[(n, w, k)][:, lo:hi].unsqueeze(2).to_broadcast([P, hi - lo, 2]),
+                    in1=table[:, FULL_TABLES.index(jt), k : k + 2, lo:hi].rearrange("p r i -> p i r"),
+                    op=ALU.mult,
+                )
+
         def multiply(unit, dst, gauss):
             n, w = unit
             jt = order[n][0]
@@ -292,10 +317,14 @@ def tile_attention_pa_kernel(tc, x, wq, wk, out_0, out_1):
             nc.gpsimd.tensor_copy(out=gate[:], in_=codes)
 
         table_whole(0, nc.vector)
+        table_small(0)
         table_frac(0)
-        table_trig(0)
+        table_first()
         for jt in range(1, TT):
             table_whole(jt, nc.gpsimd)
+        nc.gpsimd.tensor_scalar(out=plane(0, M_SIN), in0=plane(0, SIN), scalar1=-1.0, scalar2=0.0, op0=ALU.mult, op1=ALU.add)
+        for jt in range(1, TT):
+            table_small(jt)
         turn_x(0, vcopy)
         for i in range(4):
             turn_w(0, 0, i, vcopy if i + 1 < VECTOR_COPIES else scopy)
@@ -361,7 +390,12 @@ def tile_attention_pa_kernel(tc, x, wq, wk, out_0, out_1):
                     make, args = jobs[0]
                     make(*args)
                     jobs = jobs[1:]
-                multiply(units[u], prod[:, i], gauss)
+                if u == 0:
+                    multiply_part(units[u], prod[:, i], 0, HALF)
+                    nc.gpsimd.tensor_tensor(out=rot[:, 0, 0:BANK], in0=prod[:, 0, 0, 0:BANK], in1=prod[:, 0, 1, 0:BANK], op=ALU.add)
+                    multiply_part(units[u], prod[:, i], HALF, PAIRS)
+                else:
+                    multiply(units[u], prod[:, i], gauss)
                 if u == 1:
                     quantize_x(4, 4)
                     hold_gpsimd(x_codes[1][:, 3, 0:1])
@@ -379,7 +413,10 @@ def tile_attention_pa_kernel(tc, x, wq, wk, out_0, out_1):
                         finish(add([units[u]], 1, prod, rot, True, gauss))
                         finish(waiting)
                 elif split or i == 1:
-                    if split:
+                    if u == 0:
+                        nc.gpsimd.tensor_tensor(out=rot[:, 0, BANK:E], in0=prod[:, 0, 0, BANK:E], in1=prod[:, 0, 1, BANK:E], op=ALU.add)
+                        steps = [(units[u], 0, prod, rot, 0)]
+                    elif split:
                         steps = add([units[u]], i, prod, rot, on_vector(pair), gauss)
                     elif gauss and not on_vector(pair) and VRED_EVERY > 0 and pair % VRED_EVERY == VRED_PHASE:
                         steps = add([units[u - 1]], 0, prod, rot, False, gauss, True) + add([units[u]], 1, prod, rot, False, gauss)

import math
from contextlib import ExitStack

import concourse.mybir as mybir
from concourse.masks import make_identity

B, S, D, E = 4, 512, 1024, 1024
THETA = 10000.0
FLOPS = 2 * (B * S) * D * (2 * E)

F32 = mybir.dt.float32
BF16 = mybir.dt.bfloat16
I32 = mybir.dt.int32
U32 = mybir.dt.uint32
U8 = mybir.dt.uint8
FP8X4 = mybir.dt.float8_e5m2_x4
ALU = mybir.AluOpType
ACT = mybir.ActivationFunctionType

P = 128
PASSES = D // 512
PAIRS = E // 2
BANK = 512
HALF = BANK // 2
TT = S // P
NTILES = B * TT
RAW = 8
FIRST = 8
VECTOR_COPIES = 5
TURNS_A_UNIT = 3
M_SIN, COS, SIN, GA, GB = 0, 1, 2, 3, 4
GAUSS_FROM = 4
PLAIN_PAIRS = (7, 14)
VADD_FROM = 20
VADD_EVERY = 20
VRED_EVERY = 5
VRED_PHASE = 3
JOBS_FROM = 2
FULL_TABLES = (0, 1, 3)
ROTS = 3
PRODS = 4


def tile_attention_pa_kernel(tc, x, wq, wk, out_0, out_1):
    nc = tc.nc
    weights = (wq, wk)
    outs = (out_0, out_1)

    with ExitStack() as ctx:
        const = ctx.enter_context(tc.tile_pool(name="const", bufs=1))
        raw = ctx.enter_context(tc.tile_pool(name="raw", bufs=RAW))
        keep = ctx.enter_context(tc.tile_pool(name="keep", bufs=1))
        stage = ctx.enter_context(tc.tile_pool(name="stage", bufs=2))
        once = ctx.enter_context(tc.tile_pool(name="once", bufs=1))
        work = ctx.enter_context(tc.tile_pool(name="work", bufs=3))
        banks = ctx.enter_context(tc.psum_pool(name="banks", bufs=8))
        ctx.enter_context(tc.manual_schedule())

        vcopy = nc.vector.tensor_copy
        scopy = nc.scalar.copy
        order = [(jt, b) for jt in range(TT) for b in range(B)]

        theta = work.tile([P, PAIRS], F32, name="prod", bufs=PRODS)
        nc.vector.memset(theta[:, 0:1], 1.0)
        scratch = const.tile([P, 1], F32, name="scratch")
        nc.scalar.activation(out=scratch[:], in_=theta[:, 0:1], func=ACT.Sin)
        t_int = const.tile([P, TT], I32, name="t_int")
        nc.gpsimd.iota(t_int[:], pattern=[[P, TT]], base=0, channel_multiplier=1)
        ident = const.tile([P, P], F32, name="ident")
        make_identity(nc, ident[:])

        x_raw = {}
        w_raw = {}

        def load_x(n):
            jt, b = order[n]
            xr = raw.tile([P, D], BF16, name="xr")
            nc.sync.dma_start(out=xr[:], in_=x[b, jt * P : (jt + 1) * P, :])
            x_raw[n] = xr

        def load_w(w, k):
            view = weights[w].rearrange("(m q j) d -> m j q d", m=4, q=P, j=2)
            for m in range(4):
                wr = raw.tile([P, D], BF16, name="wr")
                nc.sync.dma_start(out=wr[:], in_=view[m, 1 - k])
                w_raw[(w, k, m)] = wr

        load_x(0)
        load_w(0, 0)
        load_w(0, 1)
        for n in range(1, RAW):
            load_x(n)

        n = 1
        while n < PAIRS:
            nc.vector.tensor_scalar(
                out=theta[:, n : 2 * n], in0=theta[:, 0:n],
                scalar1=THETA ** (-n / PAIRS), scalar2=None, op0=ALU.mult,
            )
            n *= 2
        halfpi = const.tile([P, 1], F32, name="halfpi")
        nc.vector.tensor_scalar(out=halfpi[:], in0=theta[:, 0:1], scalar1=math.pi / 2, scalar2=None, op0=ALU.mult)
        shifts = const.tile([P, 3], F32, name="shifts")
        for col, value in enumerate((-math.pi / 4, math.pi / 4, -math.pi / 2)):
            nc.vector.tensor_scalar(out=shifts[:, col : col + 1], in0=theta[:, 0:1], scalar1=value, scalar2=None, op0=ALU.mult)
        t_turns = const.tile([P, TT], F32, name="t_turns")
        nc.vector.tensor_scalar(out=t_turns[:], in0=t_int[:], scalar1=1.0 / (2 * math.pi), scalar2=None, op0=ALU.mult)

        table = const.tile([P, len(FULL_TABLES), 5, PAIRS], F32, name="table")
        lean = const.tile([P, TT - len(FULL_TABLES), 3, PAIRS], F32, name="lean")
        lean_tables = [jt for jt in range(TT) if jt not in FULL_TABLES]

        def plane(jt, which):
            if jt in FULL_TABLES:
                return table[:, FULL_TABLES.index(jt), which, :]
            return lean[:, lean_tables.index(jt), (COS, GA, GB).index(which), :]
        wholes = {}
        fracs = {}

        def wound(jt):
            first_small = PAIRS * math.log10((P * (jt + 1) - 1) / math.pi) / math.log10(THETA)
            return 8 * (int(first_small) // 8 + 1)

        def table_whole(jt, engine):
            whole = work.tile([P, PAIRS], I32, name="rot", bufs=ROTS)
            n = wound(jt)
            engine.tensor_scalar(out=whole[:, 0:n], in0=theta[:, 0:n], scalar1=t_turns[:, jt : jt + 1], scalar2=0.0, op0=ALU.mult, op1=ALU.add)
            wholes[jt] = whole

        def table_small(jt):
            frac = const.tile([P, PAIRS], F32, name="frac%d" % jt)
            n = wound(jt)
            nc.gpsimd.tensor_scalar(out=frac[:, n:PAIRS], in0=theta[:, n:PAIRS], scalar1=t_turns[:, jt : jt + 1], scalar2=0.0, op0=ALU.mult, op1=ALU.add)
            fracs[jt] = frac

        def table_frac(jt):
            n = wound(jt)
            nc.vector.scalar_tensor_tensor(
                out=fracs[jt][:, 0:n], in0=theta[:, 0:n], scalar=t_turns[:, jt : jt + 1], in1=wholes[jt][:, 0:n], op0=ALU.mult, op1=ALU.subtract,
            )

        def table_trig(jt):
            nc.scalar.activation(out=plane(jt, M_SIN), in_=fracs[jt][:], func=ACT.Sin, scale=-2 * math.pi)
            table_cos(jt)
            nc.scalar.activation(out=plane(jt, SIN), in_=fracs[jt][:], func=ACT.Sin, scale=2 * math.pi)

        def table_first():
            nc.scalar.activation(out=plane(0, SIN), in_=fracs[0][:], func=ACT.Sin, scale=2 * math.pi)
            table_cos(0)

        def table_sines(jt):
            nc.scalar.activation(out=plane(jt, M_SIN), in_=fracs[jt][:], func=ACT.Sin, scale=-2 * math.pi)
            nc.scalar.activation(out=plane(jt, SIN), in_=fracs[jt][:], func=ACT.Sin, scale=2 * math.pi)

        def table_cos(jt):
            absf = once.tile([P, PAIRS], F32, name="absf")
            nc.scalar.activation(out=absf[:], in_=fracs[jt][:], func=ACT.Abs)
            nc.scalar.activation(out=plane(jt, COS), in_=absf[:], func=ACT.Sin, scale=-2 * math.pi, bias=halfpi[:])

        def table_gauss(jt, h):
            absf = once.tile([P, PAIRS], F32, name="absf")
            nc.scalar.activation(out=absf[:], in_=fracs[jt][:], func=ACT.Abs, scale=2 * math.pi, bias=shifts[:, h : h + 1])
            nc.scalar.activation(out=plane(jt, GA + h), in_=absf[:], func=ACT.Sin, bias=shifts[:, 2:3])

        def turn(src, dst_words, copier):
            words = src[:].bitcast(F32)
            tp = banks.tile([P, PASSES, 2, P], F32, name="bank")
            for g in range(PASSES):
                for u in range(2):
                    nc.tensor.transpose(tp[:, g, u, :], words[:, 256 * g + u : 256 * (g + 1) : 2], ident[:])
            copier(out=dst_words, in_=tp[:].rearrange("p g u c -> p g c u"))

        x_codes = []
        x_scales = []
        for n in range(NTILES // 4):
            x_codes.append(keep.tile([P, 4, PASSES * P], U32, name="xc%d" % n, align_bytes=64))
            x_scales.append(keep.tile([P, 4, PASSES * P], U8, name="xs%d" % n, align_bytes=64))
        w_codes = {}
        w_scales = {}
        for w in range(2):
            for k in range(2):
                w_codes[(w, k)] = keep.tile([P, PASSES, BANK], U32, name="wc%d_%d" % (w, k), align_bytes=64)
                w_scales[(w, k)] = keep.tile([P, PASSES, BANK], U8, name="ws%d_%d" % (w, k), align_bytes=64)

        grouped_x = {}
        grouped_w = {}

        def turn_x(n, copier):
            if n // 4 not in grouped_x:
                gx = stage.tile([P, 4, PASSES, P, 4], BF16, name="gx", align_bytes=64)
                grouped_x[n // 4] = gx
            turn(x_raw[n], grouped_x[n // 4][:, n % 4].bitcast(F32), copier)
            if n + RAW < NTILES:
                load_x(n + RAW)

        def turn_w(w, k, m, copier):
            if (w, k) not in grouped_w:
                gw = stage.tile([P, PASSES, BANK, 4], BF16, name="gw", align_bytes=64)
                grouped_w[(w, k)] = gw
            turn(w_raw[(w, k, m)], grouped_w[(w, k)][:].bitcast(F32)[:, :, m * P : (m + 1) * P, :], copier)

        def quantize_x(first, count):
            grp, lo = first // 4, first % 4
            nc.vector.quantize_mx(
                out=x_codes[grp][:, lo : lo + count].rearrange("p n c -> p (n c)").bitcast(FP8X4),
                scales=x_scales[grp][:, lo : lo + count].rearrange("p n c -> p (n c)"),
                in_=grouped_x[grp][:, lo : lo + count].rearrange("p n g c t -> p (n g c t)"),
            )

        def quantize_w_half(w, k, half):
            cols = slice(half * HALF, (half + 1) * HALF)
            for g in range(PASSES):
                nc.vector.quantize_mx(
                    out=w_codes[(w, k)][:, g, cols].bitcast(FP8X4), scales=w_scales[(w, k)][:, g, cols],
                    in_=grouped_w[(w, k)][:, g, cols, :].rearrange("p c t -> p (c t)"),
                )

        def quantize_w(w, k):
            nc.vector.quantize_mx(
                out=w_codes[(w, k)][:].rearrange("p g c -> p (g c)").bitcast(FP8X4),
                scales=w_scales[(w, k)][:].rearrange("p g c -> p (g c)"),
                in_=grouped_w[(w, k)][:].rearrange("p g c t -> p (g c t)"),
            )

        accs = {}

        def project(unit, gauss):
            n, w = unit
            groups = [[0], [1], [0, 1]] if gauss else [[0], [1]]
            for k, parts in enumerate(groups):
                acc = banks.tile([P, BANK], F32, name="bank")
                steps = [(g, part) for g in range(PASSES) for part in parts]
                for j, (g, part) in enumerate(steps):
                    cols = slice(g * P, (g + 1) * P)
                    nc.tensor.matmul_mx(
                        out=acc[:],
                        lhsT=x_codes[n // 4][:, n % 4, cols].bitcast(FP8X4), lhsT_scale=x_scales[n // 4][:, n % 4, cols],
                        rhs=w_codes[(w, part)][:, g, :].bitcast(FP8X4), rhs_scale=w_scales[(w, part)][:, g, :],
                        start=(j == 0), stop=(j == len(steps) - 1),
                    )
                accs[(n, w, k)] = acc

        def multiply_part(unit, dst, lo, hi):
            n, w = unit
            jt = order[n][0]
            for k in range(2):
                nc.vector.tensor_tensor(
                    out=dst[:, k, 2 * lo : 2 * hi].rearrange("p (i r) -> p i r", r=2),
                    in0=accs[(n, w, k)][:, lo:hi].unsqueeze(2).to_broadcast([P, hi - lo, 2]),
                    in1=table[:, FULL_TABLES.index(jt), k : k + 2, lo:hi].rearrange("p r i -> p i r"),
                    op=ALU.mult,
                )

        def multiply(unit, dst, gauss):
            n, w = unit
            jt = order[n][0]
            for k in range(2):
                if gauss:
                    nc.vector.scalar_tensor_tensor(
                        out=dst[:, 0, k * PAIRS : (k + 1) * PAIRS], in0=accs[(n, w, k)][:], scalar=math.sqrt(2.0),
                        in1=plane(jt, GA + k), op0=ALU.mult, op1=ALU.mult,
                    )
                else:
                    nc.vector.tensor_tensor(
                        out=dst[:, k].rearrange("p (i r) -> p i r", r=2),
                        in0=accs[(n, w, k)][:].unsqueeze(2).to_broadcast([P, PAIRS, 2]),
                        in1=table[:, FULL_TABLES.index(jt), k : k + 2, :].rearrange("p r i -> p i r"),
                        op=ALU.mult,
                    )
            if gauss:
                nc.vector.tensor_tensor(out=dst[:, 1, 0:PAIRS], in0=accs[(n, w, 2)][:], in1=plane(jt, COS), op=ALU.mult)

        def add(members, lo, prod, rot, on_vector, gauss, reduce=False):
            count = len(members)
            hi = lo + count
            engine = nc.vector if on_vector else nc.gpsimd
            if not gauss:
                engine.tensor_tensor(out=rot[:, lo:hi], in0=prod[:, lo:hi, 0, :], in1=prod[:, lo:hi, 1, :], op=ALU.add)
            elif on_vector:
                for i in range(lo, hi):
                    engine.tensor_tensor(
                        out=rot[:, i].rearrange("p (i r) -> p i r", r=2),
                        in0=prod[:, i, 0, :].rearrange("p (r i) -> p i r", r=2),
                        in1=prod[:, i, 1, 0:PAIRS].unsqueeze(2).to_broadcast([P, PAIRS, 2]),
                        op=ALU.add,
                    )
            elif reduce:
                for i in range(lo, hi):
                    flat = prod[:, i].rearrange("p k e -> p (k e)")
                    for r in (1, 0):
                        nc.vector.tensor_reduce(
                            out=flat[:, (2 * r + 1) * PAIRS : (2 * r + 2) * PAIRS],
                            in_=flat[:, r * PAIRS : 2 * E - r * PAIRS].rearrange("p (j e) -> p e j", j=2)[:, 0:PAIRS, :],
                            axis=mybir.AxisListType.X, op=ALU.add,
                        )
            else:
                own = prod[:, lo:hi, 0, :].rearrange("p u (r i) -> p u r i", r=2)
                engine.tensor_tensor(
                    out=own, in0=own, in1=prod[:, lo:hi, 1, 0:PAIRS].unsqueeze(2).to_broadcast([P, count, 2, PAIRS]), op=ALU.add,
                )
            weave = 0 if on_vector or not gauss else (2 if reduce else 1)
            return [(members[i], lo + i, prod, rot, weave) for i in range(count)]

        def finish(steps):
            for (n, w), slot, prod, rot, weave in steps:
                if weave == 1:
                    scopy(out=rot[:, slot].rearrange("p (i r) -> p i r", r=2), in_=prod[:, slot, 0, :].rearrange("p (r i) -> p i r", r=2))
                if weave == 2:
                    quarters = prod[:, slot].rearrange("p k (q i) -> p i (k q)", q=2)
                    scopy(out=rot[:, slot].rearrange("p (i r) -> p i r", r=2), in_=quarters[:, :, 1::2])
                jt, b = order[n]
                nc.sync.dma_start(out=outs[w][b, jt * P : (jt + 1) * P, :], in_=rot[:, slot])

        gate = const.tile([P, 1], U32, name="gate")

        def hold_gpsimd(codes):
            nc.gpsimd.tensor_copy(out=gate[:], in_=codes)

        table_whole(0, nc.vector)
        table_small(0)
        table_frac(0)
        table_first()
        for jt in range(1, TT):
            table_whole(jt, nc.gpsimd)
        nc.gpsimd.tensor_scalar(out=plane(0, M_SIN), in0=plane(0, SIN), scalar1=-1.0, scalar2=0.0, op0=ALU.mult, op1=ALU.add)
        for jt in range(1, TT):
            table_small(jt)
        turn_x(0, vcopy)
        for i in range(4):
            turn_w(0, 0, i, vcopy if i + 1 < VECTOR_COPIES else scopy)
        load_w(1, 0)
        for jt in range(1, TT):
            table_frac(jt)
        quantize_x(0, 1)
        quantize_w_half(0, 0, 0)
        quantize_w_half(0, 0, 1)
        for m in range(4):
            turn_w(0, 1, m, scopy)
        load_w(1, 1)
        quantize_w_half(0, 1, 0)
        quantize_w_half(0, 1, 1)
        for n in range(1, 4):
            turn_x(n, scopy)
        quantize_x(1, 1)
        quantize_x(2, 2)
        table_trig(1)

        units = [(n, 0) for n in range(FIRST)] + [(n, 1) for n in range(FIRST)]
        for n in range(FIRST, NTILES):
            units.extend([(n, 0), (n, 1)])
        ahead = [("x", n) for n in range(4, FIRST)]
        ahead.extend([("w", k, m) for k in range(2) for m in range(4)])
        ahead.extend([("x", n) for n in range(FIRST, NTILES)])
        npairs = len(units) // 2

        def is_gauss(pair):
            return pair >= GAUSS_FROM and pair not in PLAIN_PAIRS

        def on_vector(pair):
            return pair == npairs - 1 or (pair >= VADD_FROM and (pair - VADD_FROM) % VADD_EVERY == 0)

        jobs = []
        for jt in range(TT):
            users = [pair for pair in range(npairs) if order[units[2 * pair][0]][0] == jt]
            if jt >= 2:
                jobs.append((table_cos, (jt,)))
            if any(is_gauss(pair) for pair in users):
                jobs.extend([(table_gauss, (jt, 0)), (table_gauss, (jt, 1))])
            if jt >= 2 and not all(is_gauss(pair) for pair in users):
                jobs.append((table_sines, (jt,)))
        waiting = []

        project(units[0], is_gauss(0))
        for pair in range(npairs):
            prod = work.tile([P, 2, 2, E], F32, name="prod", bufs=PRODS)
            rot = work.tile([P, 2, E], F32, name="rot", bufs=ROTS)
            split = pair == 0 or pair >= npairs - 2
            gauss = is_gauss(pair)
            for i in range(2):
                u = 2 * pair + i
                if u + 1 < len(units):
                    project(units[u + 1], is_gauss((u + 1) // 2))
                for step in ahead[:TURNS_A_UNIT]:
                    if step[0] == "x":
                        turn_x(step[1], scopy)
                    else:
                        turn_w(1, step[1], step[2], scopy)
                ahead = ahead[TURNS_A_UNIT:]
                if u >= JOBS_FROM and jobs:
                    make, args = jobs[0]
                    make(*args)
                    jobs = jobs[1:]
                if u == 0:
                    multiply_part(units[u], prod[:, i], 0, HALF)
                    nc.gpsimd.tensor_tensor(out=rot[:, 0, 0:BANK], in0=prod[:, 0, 0, 0:BANK], in1=prod[:, 0, 1, 0:BANK], op=ALU.add)
                    multiply_part(units[u], prod[:, i], HALF, PAIRS)
                else:
                    multiply(units[u], prod[:, i], gauss)
                if u == 1:
                    quantize_x(4, 4)
                    hold_gpsimd(x_codes[1][:, 3, 0:1])
                if u == 5:
                    quantize_w(1, 0)
                    quantize_w(1, 1)
                    hold_gpsimd(w_codes[(1, 1)][:, 1, 0:1])
                if u == 9:
                    quantize_x(8, 4)
                    quantize_x(12, 4)
                    hold_gpsimd(x_codes[3][:, 3, 0:1])
                if pair == npairs - 1:
                    if i == 1:
                        finish(add([units[u - 1]], 0, prod, rot, True, gauss))
                        finish(add([units[u]], 1, prod, rot, True, gauss))
                        finish(waiting)
                elif split or i == 1:
                    if u == 0:
                        nc.gpsimd.tensor_tensor(out=rot[:, 0, BANK:E], in0=prod[:, 0, 0, BANK:E], in1=prod[:, 0, 1, BANK:E], op=ALU.add)
                        steps = [(units[u], 0, prod, rot, 0)]
                    elif split:
                        steps = add([units[u]], i, prod, rot, on_vector(pair), gauss)
                    elif gauss and not on_vector(pair) and VRED_EVERY > 0 and pair % VRED_EVERY == VRED_PHASE:
                        steps = add([units[u - 1]], 0, prod, rot, False, gauss, True) + add([units[u]], 1, prod, rot, False, gauss)
                    else:
                        steps = add([units[u - 1], units[u]], 0, prod, rot, on_vector(pair), gauss)
                    finish(waiting)
                    waiting = []
                    if gauss and not on_vector(pair):
                        waiting = steps
                    else:
                        finish(steps)
